import numpy as np
import ml_dtypes


def mxq(x, axis, fmt="e4m3"):
    dtype, down = {"e4m3": (ml_dtypes.float8_e4m3fn, 7), "e5m2": (ml_dtypes.float8_e5m2, 14)}[fmt]
    v = np.moveaxis(np.asarray(x, np.float32).astype(ml_dtypes.bfloat16).astype(np.float64), axis, -1)
    blocks = v.reshape(v.shape[:-1] + (-1, 32))
    amax = np.abs(blocks).max(-1, keepdims=True)
    byte = np.maximum(np.where(amax > 0, np.frexp(amax)[1] - 1 + 127, 0) - down, 1)
    scale = np.exp2(byte - 127.0)
    codes = (blocks / scale).astype(np.float32).astype(dtype).astype(np.float64)
    return np.moveaxis((codes * scale).reshape(v.shape), -1, axis)


WIDE = False


def mx_kscale(k):
    if not WIDE:
        return np.ones(k)
    levels = np.array([10, -10, 5, -5, 0])
    a = np.random.permutation(np.resize(levels, k // 512 * 4)).reshape(k // 512, 4)
    idx = np.arange(k)
    return np.exp2(a[idx // 512, idx % 128 // 32])


BF16 = ml_dtypes.bfloat16


def bf(x):
    return np.asarray(x, np.float32).astype(BF16)


def f64(x):
    return np.asarray(x).astype(np.float64)


E2M1 = np.array([0.0, 0.5, 1.0, 1.5, 2.0, 3.0, 4.0, 6.0, -0.0, -0.5, -1.0, -1.5, -2.0, -3.0, -4.0, -6.0])


def pack_weight(w, fmt):
    k, n = w.shape
    w = f64(bf(w)).reshape(k // 32, 32, n)
    amax = np.abs(w).max(1)
    if fmt == "e4m3":
        byte = np.frexp(amax)[1] - 1 + 127 - 7
    else:
        mant, ex = np.frexp(amax / 6.0)
        byte = np.where(mant > 0.5, ex, ex - 1) + 127
    byte = np.clip(np.where(amax > 0, byte, 1), 1, 254)
    scaled = (w * np.exp2(127.0 - byte)[:, None, :]).reshape(k, n).astype(np.float32)
    by_word = np.ascontiguousarray(scaled.reshape(k // 512, 128, 4, n).transpose(0, 1, 3, 2))
    if fmt == "e4m3":
        words = by_word.astype(ml_dtypes.float8_e4m3fn).view(np.uint8)
    else:
        c = by_word.astype(ml_dtypes.float4_e2m1fn).view(np.uint8) & 0xF
        words = c[..., 0::2] | (c[..., 1::2] << 4)
    return np.ascontiguousarray(words), np.ascontiguousarray(byte.astype(np.uint8).reshape(k // 512, 16, n))


def unpack_weight(words, scales, fmt):
    g, p, n, _ = words.shape
    if fmt == "e4m3":
        vals = np.ascontiguousarray(words).view(ml_dtypes.float8_e4m3fn).astype(np.float64)
    else:
        nib = np.empty((g, p, n, 4), np.uint8)
        nib[..., 0::2] = words & 0xF
        nib[..., 1::2] = words >> 4
        vals = E2M1[nib]
    vals = vals * np.repeat(np.exp2(scales.astype(np.float64) - 127.0), 8, axis=1)[..., None]
    return vals.transpose(0, 1, 3, 2).reshape(g * 512, n)

def pack4(w):
    words, scales = pack_weight(w, "e2m1")
    return words.reshape(words.shape[0], 128, -1), scales


def unpack4(words, scales):
    return unpack_weight(words.reshape(words.shape[0], 128, -1, 2), scales, "e2m1")


B, DS, HH, WW, HID, HL, REP, GRP = 2, 64, 32, 32, 1024, 1024, 8, 4
C = 2 * DS
CN = REP * C


def elu(v):
    return np.where(v > 0.0, v, np.exp(np.minimum(v, 0.0)) - 1.0)


def neighbor_sum(x):
    xp = np.pad(x, ((0, 0), (0, 0), (1, 1), (1, 1)))
    full = sum(xp[:, :, di:di + HH, dj:dj + WW] for di in range(3) for dj in range(3))
    return full - x


def to_rows(t):
    return t.transpose(0, 2, 3, 1).reshape(B * HH * WW, t.shape[1])


def to_maps(r):
    return r.reshape(B, HH, WW, r.shape[1]).transpose(0, 3, 1, 2)


def setup_inputs():
    sc = mx_kscale(CN)[::REP]
    x_cat = bf(np.random.standard_normal((B, C, HH, WW)) * 0.4 * sc[None, :, None, None])
    w1 = np.random.standard_normal((HID, CN)) / np.sqrt(CN) / np.repeat(sc, REP)[None, :]
    words, scales = pack4(np.ascontiguousarray(w1.T))
    return {"x_cat": x_cat, "w1_words": words, "w1_scales": scales}


def reference(x_cat, w1_words, w1_scales):
    nbr = neighbor_sum(f64(x_cat))
    xn = np.repeat(nbr, REP, axis=1)
    z = mxq(to_rows(xn), 1, "e4m3") @ unpack4(w1_words, w1_scales)
    return to_maps(elu(z))

@@ -1,0 +1,175 @@
+from contextlib import ExitStack
+
+import concourse.mybir as mybir
+from concourse.masks import make_identity
+
+F32 = mybir.dt.float32
+BF16 = mybir.dt.bfloat16
+I32 = mybir.dt.int32
+U8 = mybir.dt.uint8
+U32 = mybir.dt.uint32
+FP8X4 = mybir.dt.float8_e4m3fn_x4
+FP4X4 = mybir.dt.float4_e2m1fn_x4
+ALU = mybir.AluOpType
+ACT = mybir.ActivationFunctionType
+
+P = 128
+PACK = 4
+BATCH, CHANNELS, ROWS, COLS = 2, 128, 32, 32
+HID = 1024
+PASSES = 2
+TILE_ROWS = 16
+N_TILE = TILE_ROWS * COLS
+PIXEL_TILES = BATCH * ROWS // TILE_ROWS
+OUT_PAIRS = HID // (2 * P)
+AHEAD = 2
+
+FLOPS = 2 * BATCH * ROWS * COLS * PASSES * P * PACK * HID
+
+
+def tile_qca_operator_deep_pa_kernel(tc, x_cat, w1_words, w1_scales, out):
+    nc = tc.nc
+    with ExitStack() as ctx:
+        ctx.enter_context(tc.manual_schedule())
+        keep = ctx.enter_context(tc.tile_pool(name="keep", bufs=1))
+        adds = ctx.enter_context(tc.tile_pool(name="adds", bufs=2))
+        stage = ctx.enter_context(tc.tile_pool(name="stage", bufs=AHEAD))
+        exps = ctx.enter_context(tc.tile_pool(name="exps", bufs=4))
+        results = ctx.enter_context(tc.tile_pool(name="results", bufs=6))
+        banks = ctx.enter_context(tc.psum_pool(name="banks", bufs=8))
+
+        x_rows = keep.tile([P, BATCH, ROWS + 2, COLS], BF16)
+        nc.vector.memset(x_rows[:, :, 0 : ROWS + 2 : ROWS + 1, :], 0.0)
+        for b in range(BATCH):
+            nc.sync.dma_start(out=x_rows[:, b, 1 : ROWS + 1, :], in_=x_cat[b])
+
+        w_words = keep.tile([P, PASSES, 2 * HID], U8, align_bytes=64)
+        for g in range(PASSES):
+            nc.sync.dma_start(out=w_words[:, g, :].bitcast(I32), in_=w1_words[g].bitcast(I32))
+
+        w_scales = keep.tile([P, PASSES, HID], U8, align_bytes=64)
+        nc.vector.memset(w_scales[:].bitcast(I32), 0)
+        for quadrant in range(4):
+            nc.sync.dma_start(
+                out=w_scales[32 * quadrant : 32 * quadrant + 4, :, :].bitcast(I32),
+                in_=w1_scales[:, 4 * quadrant : 4 * quadrant + 4, :].bitcast(I32).rearrange("g r n -> r g n"),
+            )
+
+        warm = keep.tile([P, 1], F32)
+        nc.vector.memset(warm[:], 0.0)
+        nc.scalar.activation(out=warm[:], in_=warm[:], func=ACT.Exp)
+
+        ident = keep.tile([P, P], BF16)
+        make_identity(nc, ident[:])
+        spread = keep.tile([P, 2 * CHANNELS], BF16)
+        nc.vector.tensor_copy(
+            out=spread[:].rearrange("c (k r) -> c k r", r=2),
+            in_=ident[:].unsqueeze(2).to_broadcast([P, CHANNELS, 2]),
+        )
+
+        three_rows = keep.tile([P, PIXEL_TILES, TILE_ROWS, COLS + 2], F32)
+        nc.vector.memset(three_rows[:, :, :, 0 : COLS + 2 : COLS + 1], 0.0)
+
+        nbr = keep.tile([P, PIXEL_TILES, N_TILE], BF16)
+        xn_words = keep.tile([P, PIXEL_TILES, PASSES * N_TILE], U32, align_bytes=64)
+        xn_scales = keep.tile([P, PIXEL_TILES, PASSES * N_TILE], U8, align_bytes=64)
+        grouped_of = {}
+
+        def neighbour_sum(n):
+            b, half = divmod(n, ROWS // TILE_ROWS)
+            top = TILE_ROWS * half
+            above = x_rows[:, b, top : top + TILE_ROWS, :]
+            centre = x_rows[:, b, top + 1 : top + 1 + TILE_ROWS, :]
+            below = x_rows[:, b, top + 2 : top + 2 + TILE_ROWS, :]
+            two_rows = banks.tile([P, TILE_ROWS, COLS], F32, tag="bank", name="two_rows")
+            nc.tensor.matmul(out=two_rows[:], lhsT=ident[:], rhs=above, start=True, stop=False)
+            nc.tensor.matmul(out=two_rows[:], lhsT=ident[:], rhs=below, start=False, stop=True)
+            nc.vector.tensor_tensor(
+                out=three_rows[:, n, :, 1 : COLS + 1], in0=two_rows[:], in1=centre, op=ALU.add
+            )
+            six = adds.tile([P, TILE_ROWS, COLS], F32)
+            nc.vector.tensor_tensor(
+                out=six[:],
+                in0=three_rows[:, n, :, 0:COLS],
+                in1=three_rows[:, n, :, 2 : COLS + 2],
+                op=ALU.add,
+            )
+            nc.vector.tensor_tensor(
+                out=nbr[:, n, :].rearrange("c (i j) -> c i j", j=COLS), in0=two_rows[:], in1=six[:], op=ALU.add
+            )
+
+        def spread_channels(n):
+            grouped = stage.tile([P, PASSES, PACK * N_TILE], BF16, align_bytes=64, name="grouped")
+            for g in range(PASSES):
+                twice = banks.tile([P, N_TILE, 2], BF16, tag="bank", name="twice")
+                for h in range(2):
+                    pixels = slice(h * N_TILE // 2, (h + 1) * N_TILE // 2)
+                    nc.tensor.matmul(
+                        out=twice[:, pixels, :],
+                        lhsT=spread[:, P * g : P * (g + 1)],
+                        rhs=nbr[:, n, pixels].unsqueeze(2).to_broadcast([P, N_TILE // 2, 2]),
+                        start=True,
+                        stop=True,
+                    )
+                nc.scalar.copy(
+                    out=grouped[:, g, :].bitcast(F32).rearrange("p (w d) -> p w d", d=2),
+                    in_=twice[:].bitcast(F32).to_broadcast([P, N_TILE, 2]),
+                )
+            grouped_of[n] = grouped
+
+        def quantise(n):
+            nc.vector.quantize_mx(
+                out=xn_words[:, n, :].bitcast(FP8X4),
+                scales=xn_scales[:, n, :],
+                in_=grouped_of[n][:].rearrange("p g c -> p (g c)"),
+            )
+
+        def output_pair(n, pair):
+            b, half = divmod(n, ROWS // TILE_ROWS)
+            top = TILE_ROWS * half
+            exp_m1 = exps.tile([P, 2, N_TILE], F32)
+            sums = []
+            for t in range(2):
+                m = 2 * pair + t
+                acc = banks.tile([P, N_TILE], F32, tag="bank", name="acc")
+                for g in range(PASSES):
+                    nc.tensor.matmul_mx(
+                        out=acc[:],
+                        lhsT=w_words[:, g, 2 * P * m : 2 * P * (m + 1)].bitcast(FP4X4),
+                        lhsT_scale=w_scales[:, g, P * m : P * (m + 1)],
+                        rhs=xn_words[:, n, N_TILE * g : N_TILE * (g + 1)].bitcast(FP8X4),
+                        rhs_scale=xn_scales[:, n, N_TILE * g : N_TILE * (g + 1)],
+                        start=(g == 0),
+                        stop=(g == PASSES - 1),
+                    )
+                nc.scalar.activation(out=exp_m1[:, t, :], in_=acc[:], func=ACT.Exp)
+                sums.append(acc)
+            nc.gpsimd.tensor_scalar(
+                out=exp_m1[:], in0=exp_m1[:], scalar1=1.0, scalar2=-1.0, op0=ALU.mult, op1=ALU.add
+            )
+            for t in range(2):
+                m = 2 * pair + t
+                result = results.tile([P, N_TILE], F32)
+                nc.vector.scalar_tensor_tensor(
+                    out=result[:], in0=sums[t][:], scalar=0.0, in1=exp_m1[:, t, :], op0=ALU.max, op1=ALU.min
+                )
+                nc.sync.dma_start(
+                    out=out[b, P * m : P * (m + 1), top : top + TILE_ROWS, :].rearrange("o i j -> o (i j)"),
+                    in_=result[:],
+                )
+
+        neighbour_sum(0)
+        neighbour_sum(1)
+        spread_channels(0)
+        neighbour_sum(2)
+        spread_channels(1)
+        quantise(0)
+        neighbour_sum(3)
+        quantise(1)
+        for n in range(PIXEL_TILES):
+            for pair in range(OUT_PAIRS):
+                output_pair(n, pair)
+                if n + AHEAD < PIXEL_TILES and pair == 0:
+                    spread_channels(n + AHEAD)
+                if n + AHEAD < PIXEL_TILES and pair == 2:
+                    quantise(n + AHEAD)

@@ -33,7 +33,7 @@ def tile_qca_operator_deep_pa_kernel(tc, x_cat, w1_words, w1_scales, out):
         ctx.enter_context(tc.manual_schedule())
         keep = ctx.enter_context(tc.tile_pool(name="keep", bufs=1))
         adds = ctx.enter_context(tc.tile_pool(name="adds", bufs=2))
-        stage = ctx.enter_context(tc.tile_pool(name="stage", bufs=AHEAD))
+        stage = ctx.enter_context(tc.tile_pool(name="stage", bufs=AHEAD + 1))
         exps = ctx.enter_context(tc.tile_pool(name="exps", bufs=4))
         results = ctx.enter_context(tc.tile_pool(name="results", bufs=6))
         banks = ctx.enter_context(tc.psum_pool(name="banks", bufs=8))
@@ -98,24 +98,23 @@ def tile_qca_operator_deep_pa_kernel(tc, x_cat, w1_words, w1_scales, out):
                 out=nbr[:, n, :].rearrange("c (i j) -> c i j", j=COLS), in0=two_rows[:], in1=six[:], op=ALU.add
             )
 
-        def spread_channels(n):
-            grouped = stage.tile([P, PASSES, PACK * N_TILE], BF16, align_bytes=64, name="grouped")
-            for g in range(PASSES):
-                twice = banks.tile([P, N_TILE, 2], BF16, tag="bank", name="twice")
-                for h in range(2):
-                    pixels = slice(h * N_TILE // 2, (h + 1) * N_TILE // 2)
-                    nc.tensor.matmul(
-                        out=twice[:, pixels, :],
-                        lhsT=spread[:, P * g : P * (g + 1)],
-                        rhs=nbr[:, n, pixels].unsqueeze(2).to_broadcast([P, N_TILE // 2, 2]),
-                        start=True,
-                        stop=True,
-                    )
-                nc.scalar.copy(
-                    out=grouped[:, g, :].bitcast(F32).rearrange("p (w d) -> p w d", d=2),
-                    in_=twice[:].bitcast(F32).to_broadcast([P, N_TILE, 2]),
+        def spread_channels(n, g, copy):
+            if g == 0:
+                grouped_of[n] = stage.tile([P, PASSES, PACK * N_TILE], BF16, align_bytes=64, name="grouped")
+            twice = banks.tile([P, N_TILE, 2], BF16, tag="bank", name="twice")
+            for h in range(2):
+                pixels = slice(h * N_TILE // 2, (h + 1) * N_TILE // 2)
+                nc.tensor.matmul(
+                    out=twice[:, pixels, :],
+                    lhsT=spread[:, P * g : P * (g + 1)],
+                    rhs=nbr[:, n, pixels].unsqueeze(2).to_broadcast([P, N_TILE // 2, 2]),
+                    start=True,
+                    stop=True,
                 )
-            grouped_of[n] = grouped
+            copy(
+                out=grouped_of[n][:, g, :].bitcast(F32).rearrange("p (w d) -> p w d", d=2),
+                in_=twice[:].bitcast(F32).to_broadcast([P, N_TILE, 2]),
+            )
 
         def quantise(n):
             nc.vector.quantize_mx(
@@ -160,16 +159,20 @@ def tile_qca_operator_deep_pa_kernel(tc, x_cat, w1_words, w1_scales, out):
 
         neighbour_sum(0)
         neighbour_sum(1)
-        spread_channels(0)
+        for g in range(PASSES):
+            spread_channels(0, g, nc.scalar.copy)
         neighbour_sum(2)
-        spread_channels(1)
+        for g in range(PASSES):
+            spread_channels(1, g, nc.scalar.copy)
         quantise(0)
         neighbour_sum(3)
         quantise(1)
+        for g in range(PASSES):
+            spread_channels(2, g, nc.vector.tensor_copy)
+        last = PIXEL_TILES - 1
         for n in range(PIXEL_TILES):
             for pair in range(OUT_PAIRS):
                 output_pair(n, pair)
-                if n + AHEAD < PIXEL_TILES and pair == 0:
-                    spread_channels(n + AHEAD)
-                if n + AHEAD < PIXEL_TILES and pair == 2:
+                if pair == 1 and n < PASSES:
+                    spread_channels(last, n, nc.scalar.copy)
                     quantise(n + AHEAD)

@@ -75,28 +75,39 @@ def tile_qca_operator_deep_pa_kernel(tc, x_cat, w1_words, w1_scales, out):
         xn_scales = keep.tile([P, PIXEL_TILES, PASSES * N_TILE], U8, align_bytes=64)
         grouped_of = {}
 
-        def neighbour_sum(n):
+        centre_of, two_rows_of = {}, {}
+
+        def rows_above_and_below(n):
             b, half = divmod(n, ROWS // TILE_ROWS)
             top = TILE_ROWS * half
             above = x_rows[:, b, top : top + TILE_ROWS, :]
-            centre = x_rows[:, b, top + 1 : top + 1 + TILE_ROWS, :]
+            centre_of[n] = x_rows[:, b, top + 1 : top + 1 + TILE_ROWS, :]
             below = x_rows[:, b, top + 2 : top + 2 + TILE_ROWS, :]
-            two_rows = banks.tile([P, TILE_ROWS, COLS], F32, tag="bank", name="two_rows")
-            nc.tensor.matmul(out=two_rows[:], lhsT=ident[:], rhs=above, start=True, stop=False)
-            nc.tensor.matmul(out=two_rows[:], lhsT=ident[:], rhs=below, start=False, stop=True)
-            nc.vector.tensor_tensor(
-                out=three_rows[:, n, :, 1 : COLS + 1], in0=two_rows[:], in1=centre, op=ALU.add
-            )
-            six = adds.tile([P, TILE_ROWS, COLS], F32)
-            nc.vector.tensor_tensor(
-                out=six[:],
-                in0=three_rows[:, n, :, 0:COLS],
-                in1=three_rows[:, n, :, 2 : COLS + 2],
-                op=ALU.add,
-            )
-            nc.vector.tensor_tensor(
-                out=nbr[:, n, :].rearrange("c (i j) -> c i j", j=COLS), in0=two_rows[:], in1=six[:], op=ALU.add
-            )
+            two_rows_of[n] = banks.tile([P, TILE_ROWS, COLS], F32, tag="bank", name="two_rows")
+            nc.tensor.matmul(out=two_rows_of[n][:], lhsT=ident[:], rhs=above, start=True, stop=False)
+            nc.tensor.matmul(out=two_rows_of[n][:], lhsT=ident[:], rhs=below, start=False, stop=True)
+
+        def neighbour_sums(tiles):
+            six_of = {}
+            for n in tiles:
+                nc.vector.tensor_tensor(
+                    out=three_rows[:, n, :, 1 : COLS + 1], in0=two_rows_of[n][:], in1=centre_of[n], op=ALU.add
+                )
+            for n in tiles:
+                six_of[n] = adds.tile([P, TILE_ROWS, COLS], F32, name="six")
+                nc.vector.tensor_tensor(
+                    out=six_of[n][:],
+                    in0=three_rows[:, n, :, 0:COLS],
+                    in1=three_rows[:, n, :, 2 : COLS + 2],
+                    op=ALU.add,
+                )
+            for n in tiles:
+                nc.vector.tensor_tensor(
+                    out=nbr[:, n, :].rearrange("c (i j) -> c i j", j=COLS),
+                    in0=two_rows_of[n][:],
+                    in1=six_of[n][:],
+                    op=ALU.add,
+                )
 
         def spread_channels(n, g, copy):
             if g == 0:
@@ -157,15 +168,15 @@ def tile_qca_operator_deep_pa_kernel(tc, x_cat, w1_words, w1_scales, out):
                     in_=result[:],
                 )
 
-        neighbour_sum(0)
-        neighbour_sum(1)
+        for n in range(PIXEL_TILES):
+            rows_above_and_below(n)
+        neighbour_sums((0, 1))
         for g in range(PASSES):
             spread_channels(0, g, nc.scalar.copy)
-        neighbour_sum(2)
+        neighbour_sums((2, 3))
         for g in range(PASSES):
             spread_channels(1, g, nc.scalar.copy)
         quantise(0)
-        neighbour_sum(3)
         quantise(1)
         for g in range(PASSES):
             spread_channels(2, g, nc.vector.tensor_copy)

@@ -40,8 +40,9 @@ def tile_qca_operator_deep_pa_kernel(tc, x_cat, w1_words, w1_scales, out):
 
         x_rows = keep.tile([P, BATCH, ROWS + 2, COLS], BF16)
         nc.vector.memset(x_rows[:, :, 0 : ROWS + 2 : ROWS + 1, :], 0.0)
-        for b in range(BATCH):
-            nc.sync.dma_start(out=x_rows[:, b, 1 : ROWS + 1, :], in_=x_cat[b])
+        nc.sync.dma_start(out=x_rows[:, 0, 1 : TILE_ROWS + 2, :], in_=x_cat[0, :, 0 : TILE_ROWS + 1, :])
+        nc.sync.dma_start(out=x_rows[:, 0, TILE_ROWS + 2 : ROWS + 1, :], in_=x_cat[0, :, TILE_ROWS + 1 : ROWS, :])
+        nc.sync.dma_start(out=x_rows[:, 1, 1 : ROWS + 1, :], in_=x_cat[1])
 
         w_words = keep.tile([P, PASSES, 2 * HID], U8, align_bytes=64)
         for g in range(PASSES):
@@ -134,7 +135,12 @@ def tile_qca_operator_deep_pa_kernel(tc, x_cat, w1_words, w1_scales, out):
                 in_=grouped_of[n][:].rearrange("p g c -> p (g c)"),
             )
 
-        def output_pair(n, pair):
+        def minus_one(exp_of_sums):
+            nc.gpsimd.tensor_scalar(
+                out=exp_of_sums, in0=exp_of_sums, scalar1=1.0, scalar2=-1.0, op0=ALU.mult, op1=ALU.add
+            )
+
+        def output_pair(n, pair, tile_by_tile):
             b, half = divmod(n, ROWS // TILE_ROWS)
             top = TILE_ROWS * half
             exp_m1 = exps.tile([P, 2, N_TILE], F32)
@@ -154,19 +160,31 @@ def tile_qca_operator_deep_pa_kernel(tc, x_cat, w1_words, w1_scales, out):
                     )
                 nc.scalar.activation(out=exp_m1[:, t, :], in_=acc[:], func=ACT.Exp)
                 sums.append(acc)
-            nc.gpsimd.tensor_scalar(
-                out=exp_m1[:], in0=exp_m1[:], scalar1=1.0, scalar2=-1.0, op0=ALU.mult, op1=ALU.add
-            )
+                if tile_by_tile:
+                    minus_one(exp_m1[:, t, :])
+            if not tile_by_tile:
+                minus_one(exp_m1[:])
             for t in range(2):
                 m = 2 * pair + t
                 result = results.tile([P, N_TILE], F32)
-                nc.vector.scalar_tensor_tensor(
-                    out=result[:], in0=sums[t][:], scalar=0.0, in1=exp_m1[:, t, :], op0=ALU.max, op1=ALU.min
-                )
-                nc.sync.dma_start(
-                    out=out[b, P * m : P * (m + 1), top : top + TILE_ROWS, :].rearrange("o i j -> o (i j)"),
-                    in_=result[:],
-                )
+                pieces = 2 if (n, m) == (PIXEL_TILES - 1, HID // P - 1) else 1
+                rows = TILE_ROWS // pieces
+                for piece in range(pieces):
+                    columns = slice(piece * rows * COLS, (piece + 1) * rows * COLS)
+                    nc.vector.scalar_tensor_tensor(
+                        out=result[:, columns],
+                        in0=sums[t][:, columns],
+                        scalar=0.0,
+                        in1=exp_m1[:, t, columns],
+                        op0=ALU.max,
+                        op1=ALU.min,
+                    )
+                    nc.sync.dma_start(
+                        out=out[
+                            b, P * m : P * (m + 1), top + piece * rows : top + (piece + 1) * rows, :
+                        ].rearrange("o i j -> o (i j)"),
+                        in_=result[:, columns],
+                    )
 
         for n in range(PIXEL_TILES):
             rows_above_and_below(n)
@@ -183,7 +201,7 @@ def tile_qca_operator_deep_pa_kernel(tc, x_cat, w1_words, w1_scales, out):
         last = PIXEL_TILES - 1
         for n in range(PIXEL_TILES):
             for pair in range(OUT_PAIRS):
-                output_pair(n, pair)
+                output_pair(n, pair, (n, pair) in ((0, 0), (PIXEL_TILES - 1, OUT_PAIRS - 1)))
                 if pair == 1 and n < PASSES:
                     spread_channels(last, n, nc.scalar.copy)
                     quantise(n + AHEAD)

@@ -35,7 +35,7 @@ def tile_qca_operator_deep_pa_kernel(tc, x_cat, w1_words, w1_scales, out):
         adds = ctx.enter_context(tc.tile_pool(name="adds", bufs=2))
         stage = ctx.enter_context(tc.tile_pool(name="stage", bufs=AHEAD + 1))
         exps = ctx.enter_context(tc.tile_pool(name="exps", bufs=4))
-        results = ctx.enter_context(tc.tile_pool(name="results", bufs=6))
+        results = ctx.enter_context(tc.tile_pool(name="results", bufs=4))
         banks = ctx.enter_context(tc.psum_pool(name="banks", bufs=8))
 
         x_rows = keep.tile([P, BATCH, ROWS + 2, COLS], BF16)
@@ -164,27 +164,36 @@ def tile_qca_operator_deep_pa_kernel(tc, x_cat, w1_words, w1_scales, out):
                     minus_one(exp_m1[:, t, :])
             if not tile_by_tile:
                 minus_one(exp_m1[:])
+            result = results.tile([P, 2, N_TILE], F32)
+            final_pair = (n, pair) == (PIXEL_TILES - 1, OUT_PAIRS - 1)
             for t in range(2):
                 m = 2 * pair + t
-                result = results.tile([P, N_TILE], F32)
-                pieces = 2 if (n, m) == (PIXEL_TILES - 1, HID // P - 1) else 1
+                pieces = 2 if final_pair and t == 1 else 1
                 rows = TILE_ROWS // pieces
                 for piece in range(pieces):
                     columns = slice(piece * rows * COLS, (piece + 1) * rows * COLS)
                     nc.vector.scalar_tensor_tensor(
-                        out=result[:, columns],
+                        out=result[:, t, columns],
                         in0=sums[t][:, columns],
                         scalar=0.0,
                         in1=exp_m1[:, t, columns],
                         op0=ALU.max,
                         op1=ALU.min,
                     )
-                    nc.sync.dma_start(
-                        out=out[
-                            b, P * m : P * (m + 1), top + piece * rows : top + (piece + 1) * rows, :
-                        ].rearrange("o i j -> o (i j)"),
-                        in_=result[:, columns],
-                    )
+                    if final_pair:
+                        nc.sync.dma_start(
+                            out=out[
+                                b, P * m : P * (m + 1), top + piece * rows : top + (piece + 1) * rows, :
+                            ].rearrange("o i j -> o (i j)"),
+                            in_=result[:, t, columns],
+                        )
+            if not final_pair:
+                nc.sync.dma_start(
+                    out=out[b, 2 * P * pair : 2 * P * (pair + 1), top : top + TILE_ROWS, :].rearrange(
+                        "(t o) i j -> o t (i j)", t=2
+                    ),
+                    in_=result[:],
+                )
 
         for n in range(PIXEL_TILES):
             rows_above_and_below(n)

@@ -18,7 +18,10 @@ PACK = 4
 BATCH, CHANNELS, ROWS, COLS = 2, 128, 32, 32
 HID = 1024
 PASSES = 2
+BLOCK_ROWS = P // COLS
+OUT_ROWS = BLOCK_ROWS - 2
 TILE_ROWS = 16
+BLOCKS = TILE_ROWS // OUT_ROWS
 N_TILE = TILE_ROWS * COLS
 PIXEL_TILES = BATCH * ROWS // TILE_ROWS
 OUT_PAIRS = HID // (2 * P)
@@ -32,12 +35,15 @@ def tile_qca_operator_deep_pa_kernel(tc, x_cat, w1_words, w1_scales, out):
     with ExitStack() as ctx:
         ctx.enter_context(tc.manual_schedule())
         keep = ctx.enter_context(tc.tile_pool(name="keep", bufs=1))
-        adds = ctx.enter_context(tc.tile_pool(name="adds", bufs=2))
-        stage = ctx.enter_context(tc.tile_pool(name="stage", bufs=AHEAD + 1))
+        stage = ctx.enter_context(tc.tile_pool(name="stage", bufs=PIXEL_TILES))
         exps = ctx.enter_context(tc.tile_pool(name="exps", bufs=4))
         results = ctx.enter_context(tc.tile_pool(name="results", bufs=4))
         banks = ctx.enter_context(tc.psum_pool(name="banks", bufs=8))
 
+        ident = keep.tile([P, P], BF16)
+        make_identity(nc, ident[:])
+        zeros = keep.tile([P, P], BF16)
+        nc.vector.memset(zeros[:], 0.0)
         x_rows = keep.tile([P, BATCH, ROWS + 2, COLS], BF16)
         nc.vector.memset(x_rows[:, :, 0 : ROWS + 2 : ROWS + 1, :], 0.0)
         nc.sync.dma_start(out=x_rows[:, 0, 1 : TILE_ROWS + 2, :], in_=x_cat[0, :, 0 : TILE_ROWS + 1, :])
@@ -49,7 +55,7 @@ def tile_qca_operator_deep_pa_kernel(tc, x_cat, w1_words, w1_scales, out):
             nc.sync.dma_start(out=w_words[:, g, :].bitcast(I32), in_=w1_words[g].bitcast(I32))
 
         w_scales = keep.tile([P, PASSES, HID], U8, align_bytes=64)
-        nc.vector.memset(w_scales[:].bitcast(I32), 0)
+        nc.gpsimd.memset(w_scales[:].bitcast(I32), 0)
         for quadrant in range(4):
             nc.sync.dma_start(
                 out=w_scales[32 * quadrant : 32 * quadrant + 4, :, :].bitcast(I32),
@@ -60,73 +66,126 @@ def tile_qca_operator_deep_pa_kernel(tc, x_cat, w1_words, w1_scales, out):
         nc.vector.memset(warm[:], 0.0)
         nc.scalar.activation(out=warm[:], in_=warm[:], func=ACT.Exp)
 
-        ident = keep.tile([P, P], BF16)
-        make_identity(nc, ident[:])
-        spread = keep.tile([P, 2 * CHANNELS], BF16)
+        idle = banks.tile([P, N_TILE], F32, tag="bank", name="idle")
+        for w in range(3):
+            nc.tensor.matmul(
+                out=idle[:], lhsT=zeros[:], rhs=zeros[:, 0:1].to_broadcast([P, N_TILE]), start=True, stop=True
+            )
+
+        mixed = keep.tile([P, P], BF16)
         nc.vector.tensor_copy(
-            out=spread[:].rearrange("c (k r) -> c k r", r=2),
-            in_=ident[:].unsqueeze(2).to_broadcast([P, CHANNELS, 2]),
+            out=mixed[:].rearrange("c (k g) -> c g k", g=PASSES), in_=ident[:].rearrange("c (g k) -> c g k", g=PASSES)
+        )
+        spread = keep.tile([P, PASSES, CHANNELS], BF16)
+        nc.vector.tensor_copy(
+            out=spread[:].rearrange("m g (k r) -> m g k r", r=2),
+            in_=ident[:].rearrange("m (k g) -> m g k", g=PASSES).unsqueeze(3).to_broadcast([P, PASSES, CHANNELS // 2, 2]),
         )
 
-        three_rows = keep.tile([P, PIXEL_TILES, TILE_ROWS, COLS + 2], F32)
-        nc.vector.memset(three_rows[:, :, :, 0 : COLS + 2 : COLS + 1], 0.0)
+        pixel = ident[:].rearrange("k (i j) -> k i j", j=COLS)
+        three = keep.tile([P, OUT_ROWS, COLS + 2], BF16)
+        nc.vector.memset(three[:, :, 0 : COLS + 2 : COLS + 1], 0.0)
+        two = keep.tile([P, OUT_ROWS, COLS], BF16)
+        nc.vector.tensor_tensor(out=two[:], in0=pixel[:, 0:2, :], in1=pixel[:, 2:4, :], op=ALU.add)
+        nc.vector.tensor_tensor(out=three[:, :, 1 : COLS + 1], in0=two[:], in1=pixel[:, 1:3, :], op=ALU.add)
+        sides = keep.tile([P, OUT_ROWS, COLS], BF16)
+        nc.vector.tensor_tensor(
+            out=sides[:], in0=three[:, :, 0:COLS], in1=three[:, :, 2 : COLS + 2], op=ALU.add
+        )
+        window = keep.tile([P, OUT_ROWS * COLS], BF16)
+        nc.vector.tensor_tensor(
+            out=window[:].rearrange("k (i j) -> k i j", j=COLS), in0=sides[:], in1=two[:], op=ALU.add
+        )
 
+        x_turned = keep.tile([P, PIXEL_TILES, BLOCKS, P], BF16)
         nbr = keep.tile([P, PIXEL_TILES, N_TILE], BF16)
         xn_words = keep.tile([P, PIXEL_TILES, PASSES * N_TILE], U32, align_bytes=64)
         xn_scales = keep.tile([P, PIXEL_TILES, PASSES * N_TILE], U8, align_bytes=64)
         grouped_of = {}
 
-        centre_of, two_rows_of = {}, {}
+        turned_of, summed_of = {}, {}
 
-        def rows_above_and_below(n):
+        def turn(n, part, parts):
             b, half = divmod(n, ROWS // TILE_ROWS)
             top = TILE_ROWS * half
-            above = x_rows[:, b, top : top + TILE_ROWS, :]
-            centre_of[n] = x_rows[:, b, top + 1 : top + 1 + TILE_ROWS, :]
-            below = x_rows[:, b, top + 2 : top + 2 + TILE_ROWS, :]
-            two_rows_of[n] = banks.tile([P, TILE_ROWS, COLS], F32, tag="bank", name="two_rows")
-            nc.tensor.matmul(out=two_rows_of[n][:], lhsT=ident[:], rhs=above, start=True, stop=False)
-            nc.tensor.matmul(out=two_rows_of[n][:], lhsT=ident[:], rhs=below, start=False, stop=True)
-
-        def neighbour_sums(tiles):
-            six_of = {}
-            for n in tiles:
-                nc.vector.tensor_tensor(
-                    out=three_rows[:, n, :, 1 : COLS + 1], in0=two_rows_of[n][:], in1=centre_of[n], op=ALU.add
-                )
-            for n in tiles:
-                six_of[n] = adds.tile([P, TILE_ROWS, COLS], F32, name="six")
-                nc.vector.tensor_tensor(
-                    out=six_of[n][:],
-                    in0=three_rows[:, n, :, 0:COLS],
-                    in1=three_rows[:, n, :, 2 : COLS + 2],
-                    op=ALU.add,
-                )
-            for n in tiles:
-                nc.vector.tensor_tensor(
-                    out=nbr[:, n, :].rearrange("c (i j) -> c i j", j=COLS),
-                    in0=two_rows_of[n][:],
-                    in1=six_of[n][:],
-                    op=ALU.add,
+            count = BLOCKS // parts
+            turned_of[n, part] = banks.tile([P, count, P], BF16, tag="bank", name="turned")
+            for i in range(count):
+                first = top + OUT_ROWS * (part * count + i)
+                nc.tensor.transpose(
+                    turned_of[n, part][:, i, :],
+                    x_rows[:, b, first : first + BLOCK_ROWS, :].rearrange("c i j -> c (i j)"),
+                    mixed[:],
                 )
 
-        def spread_channels(n, g, copy):
-            if g == 0:
-                grouped_of[n] = stage.tile([P, PASSES, PACK * N_TILE], BF16, align_bytes=64, name="grouped")
-            twice = banks.tile([P, N_TILE, 2], BF16, tag="bank", name="twice")
+        def keep_turned(n, part, parts, copy):
+            count = BLOCKS // parts
+            copy(
+                out=x_turned[:, n, part * count : (part + 1) * count, :]
+                .rearrange("k i c -> k (i c)")
+                .bitcast(F32),
+                in_=turned_of[n, part][:].rearrange("k i c -> k (i c)").bitcast(F32),
+            )
+
+        def sum_neighbours(n):
+            summed_of[n] = banks.tile([P, N_TILE], BF16, tag="bank", name="summed")
+            width = OUT_ROWS * COLS
+            for i in range(BLOCKS):
+                nc.tensor.matmul(
+                    out=summed_of[n][:, width * i : width * (i + 1)],
+                    lhsT=x_turned[:, n, i, :],
+                    rhs=window[:],
+                    start=True,
+                    stop=True,
+                )
+
+        def keep_summed(n, copy):
+            copy(out=nbr[:, n, :].bitcast(F32), in_=summed_of[n][:].bitcast(F32))
+
+        twice_of = {}
+
+        def spread_channels(n, g):
+            twice_of[n, g] = banks.tile([P, N_TILE, 2], BF16, tag="bank", name="twice")
             for h in range(2):
                 pixels = slice(h * N_TILE // 2, (h + 1) * N_TILE // 2)
                 nc.tensor.matmul(
-                    out=twice[:, pixels, :],
-                    lhsT=spread[:, P * g : P * (g + 1)],
+                    out=twice_of[n, g][:, pixels, :],
+                    lhsT=spread[:, g, :],
                     rhs=nbr[:, n, pixels].unsqueeze(2).to_broadcast([P, N_TILE // 2, 2]),
                     start=True,
                     stop=True,
                 )
+
+        def make_words(n, g, copy):
+            if g == 0:
+                grouped_of[n] = stage.tile([P, PASSES, PACK * N_TILE], BF16, align_bytes=64, name="grouped")
             copy(
                 out=grouped_of[n][:, g, :].bitcast(F32).rearrange("p (w d) -> p w d", d=2),
-                in_=twice[:].bitcast(F32).to_broadcast([P, N_TILE, 2]),
+                in_=twice_of[n, g][:].bitcast(F32).to_broadcast([P, N_TILE, 2]),
             )
+
+        def sum_neighbours_twice(n):
+            summed_of[n] = banks.tile([P, N_TILE, 2], BF16, tag="bank", name="summed")
+            width = OUT_ROWS * COLS
+            for i in range(BLOCKS):
+                nc.tensor.matmul(
+                    out=summed_of[n][:, width * i : width * (i + 1), :],
+                    lhsT=x_turned[:, n, i, :],
+                    rhs=window[:].unsqueeze(2).to_broadcast([P, width, 2]),
+                    start=True,
+                    stop=True,
+                )
+
+        def move_words(n, copy):
+            grouped_of[n] = stage.tile([P, PASSES, PACK * N_TILE], BF16, align_bytes=64, name="grouped")
+            quads = stage.tile([P, PACK * N_TILE], BF16, name="quads")
+            copy(
+                out=quads[:].bitcast(F32).rearrange("m (w d) -> m w d", d=2),
+                in_=summed_of[n][:].bitcast(F32).to_broadcast([P, N_TILE, 2]),
+            )
+            for g in range(PASSES):
+                for r in range(2):
+                    nc.sync.dma_start(out=grouped_of[n][r:P:2, g, :], in_=quads[g:P:2, :])
 
         def quantise(n):
             nc.vector.quantize_mx(
@@ -195,22 +254,36 @@ def tile_qca_operator_deep_pa_kernel(tc, x_cat, w1_words, w1_scales, out):
                     in_=result[:],
                 )
 
-        for n in range(PIXEL_TILES):
-            rows_above_and_below(n)
-        neighbour_sums((0, 1))
-        for g in range(PASSES):
-            spread_channels(0, g, nc.scalar.copy)
-        neighbour_sums((2, 3))
-        for g in range(PASSES):
-            spread_channels(1, g, nc.scalar.copy)
+        scalar, vector = nc.scalar.copy, nc.vector.tensor_copy
+        turn(0, 0, 1)
+        turn(1, 0, 1)
+        turn(2, 0, 1)
+        keep_turned(0, 0, 1, scalar)
+        keep_turned(1, 0, 1, vector)
+        sum_neighbours(0)
+        turn(3, 0, 1)
+        keep_turned(2, 0, 1, scalar)
+        keep_summed(0, scalar)
+        sum_neighbours_twice(2)
+        spread_channels(0, 0)
+        spread_channels(0, 1)
+        keep_turned(3, 0, 1, vector)
+        move_words(2, vector)
+        make_words(0, 0, scalar)
+        sum_neighbours(1)
+        make_words(0, 1, vector)
         quantise(0)
+        sum_neighbours_twice(3)
+        keep_summed(1, scalar)
+        move_words(3, scalar)
+        spread_channels(1, 0)
+        spread_channels(1, 1)
+        make_words(1, 0, scalar)
+        make_words(1, 1, vector)
         quantise(1)
-        for g in range(PASSES):
-            spread_channels(2, g, nc.vector.tensor_copy)
-        last = PIXEL_TILES - 1
+        quantise(2)
         for n in range(PIXEL_TILES):
             for pair in range(OUT_PAIRS):
                 output_pair(n, pair, (n, pair) in ((0, 0), (PIXEL_TILES - 1, OUT_PAIRS - 1)))
-                if pair == 1 and n < PASSES:
-                    spread_channels(last, n, nc.scalar.copy)
-                    quantise(n + AHEAD)
+                if (n, pair) == (1, 0):
+                    quantise(3)

@@ -281,9 +281,8 @@ def tile_qca_operator_deep_pa_kernel(tc, x_cat, w1_words, w1_scales, out):
         make_words(1, 0, scalar)
         make_words(1, 1, vector)
         quantise(1)
-        quantise(2)
         for n in range(PIXEL_TILES):
             for pair in range(OUT_PAIRS):
                 output_pair(n, pair, (n, pair) in ((0, 0), (PIXEL_TILES - 1, OUT_PAIRS - 1)))
-                if (n, pair) == (1, 0):
-                    quantise(3)
+                if pair == 2 and n < AHEAD:
+                    quantise(n + AHEAD)

@@ -36,8 +36,8 @@ def tile_qca_operator_deep_pa_kernel(tc, x_cat, w1_words, w1_scales, out):
         ctx.enter_context(tc.manual_schedule())
         keep = ctx.enter_context(tc.tile_pool(name="keep", bufs=1))
         stage = ctx.enter_context(tc.tile_pool(name="stage", bufs=PIXEL_TILES))
-        exps = ctx.enter_context(tc.tile_pool(name="exps", bufs=4))
-        results = ctx.enter_context(tc.tile_pool(name="results", bufs=4))
+        exps = ctx.enter_context(tc.tile_pool(name="exps", bufs=6))
+        results = ctx.enter_context(tc.tile_pool(name="results", bufs=8))
         banks = ctx.enter_context(tc.psum_pool(name="banks", bufs=8))
 
         ident = keep.tile([P, P], BF16)
@@ -200,6 +200,7 @@ def tile_qca_operator_deep_pa_kernel(tc, x_cat, w1_words, w1_scales, out):
             )
 
         def output_pair(n, pair, tile_by_tile):
+            while_quantising = pair == 0 and n in (1, 2)
             b, half = divmod(n, ROWS // TILE_ROWS)
             top = TILE_ROWS * half
             exp_m1 = exps.tile([P, 2, N_TILE], F32)
@@ -221,7 +222,9 @@ def tile_qca_operator_deep_pa_kernel(tc, x_cat, w1_words, w1_scales, out):
                 sums.append(acc)
                 if tile_by_tile:
                     minus_one(exp_m1[:, t, :])
-            if not tile_by_tile:
+            if while_quantising:
+                nc.scalar.activation(out=exp_m1[:], in_=exp_m1[:], func=ACT.Copy, bias=-1.0)
+            elif not tile_by_tile:
                 minus_one(exp_m1[:])
             result = results.tile([P, 2, N_TILE], F32)
             final_pair = (n, pair) == (PIXEL_TILES - 1, OUT_PAIRS - 1)

@@ -16,18 +16,17 @@ ACT = mybir.ActivationFunctionType
 P = 128
 PACK = 4
 BATCH, CHANNELS, ROWS, COLS = 2, 128, 32, 32
+PIXELS = BATCH * ROWS * COLS
 HID = 1024
 PASSES = 2
 BLOCK_ROWS = P // COLS
 OUT_ROWS = BLOCK_ROWS - 2
-TILE_ROWS = 16
-BLOCKS = TILE_ROWS // OUT_ROWS
-N_TILE = TILE_ROWS * COLS
-PIXEL_TILES = BATCH * ROWS // TILE_ROWS
-OUT_PAIRS = HID // (2 * P)
-AHEAD = 2
+OUT_PIXELS = OUT_ROWS * COLS
+BANK = 512
+TILES = ((0, 0, 8), (0, 8, 8), (0, 16, 16), (1, 0, 16), (1, 16, 16))
+UNITS = PIXELS * HID // (P * 2 * BANK)
 
-FLOPS = 2 * BATCH * ROWS * COLS * PASSES * P * PACK * HID
+FLOPS = 2 * PIXELS * PASSES * P * PACK * HID
 
 
 def tile_qca_operator_deep_pa_kernel(tc, x_cat, w1_words, w1_scales, out):
@@ -35,7 +34,6 @@ def tile_qca_operator_deep_pa_kernel(tc, x_cat, w1_words, w1_scales, out):
     with ExitStack() as ctx:
         ctx.enter_context(tc.manual_schedule())
         keep = ctx.enter_context(tc.tile_pool(name="keep", bufs=1))
-        stage = ctx.enter_context(tc.tile_pool(name="stage", bufs=PIXEL_TILES))
         exps = ctx.enter_context(tc.tile_pool(name="exps", bufs=6))
         results = ctx.enter_context(tc.tile_pool(name="results", bufs=8))
         banks = ctx.enter_context(tc.psum_pool(name="banks", bufs=8))
@@ -46,8 +44,9 @@ def tile_qca_operator_deep_pa_kernel(tc, x_cat, w1_words, w1_scales, out):
         nc.vector.memset(zeros[:], 0.0)
         x_rows = keep.tile([P, BATCH, ROWS + 2, COLS], BF16)
         nc.vector.memset(x_rows[:, :, 0 : ROWS + 2 : ROWS + 1, :], 0.0)
-        nc.sync.dma_start(out=x_rows[:, 0, 1 : TILE_ROWS + 2, :], in_=x_cat[0, :, 0 : TILE_ROWS + 1, :])
-        nc.sync.dma_start(out=x_rows[:, 0, TILE_ROWS + 2 : ROWS + 1, :], in_=x_cat[0, :, TILE_ROWS + 1 : ROWS, :])
+        first = 17
+        nc.sync.dma_start(out=x_rows[:, 0, 1 : first + 1, :], in_=x_cat[0, :, 0:first, :])
+        nc.sync.dma_start(out=x_rows[:, 0, first + 1 : ROWS + 1, :], in_=x_cat[0, :, first:ROWS, :])
         nc.sync.dma_start(out=x_rows[:, 1, 1 : ROWS + 1, :], in_=x_cat[1])
 
         w_words = keep.tile([P, PASSES, 2 * HID], U8, align_bytes=64)
@@ -66,22 +65,14 @@ def tile_qca_operator_deep_pa_kernel(tc, x_cat, w1_words, w1_scales, out):
         nc.vector.memset(warm[:], 0.0)
         nc.scalar.activation(out=warm[:], in_=warm[:], func=ACT.Exp)
 
-        idle = banks.tile([P, N_TILE], F32, tag="bank", name="idle")
+        idle = banks.tile([P, BANK], F32, tag="bank", name="idle")
         for w in range(3):
-            nc.tensor.matmul(
-                out=idle[:], lhsT=zeros[:], rhs=zeros[:, 0:1].to_broadcast([P, N_TILE]), start=True, stop=True
-            )
+            nc.tensor.matmul(out=idle[:], lhsT=zeros[:], rhs=zeros[:, 0:1].to_broadcast([P, BANK]), start=True, stop=True)
 
         mixed = keep.tile([P, P], BF16)
         nc.vector.tensor_copy(
             out=mixed[:].rearrange("c (k g) -> c g k", g=PASSES), in_=ident[:].rearrange("c (g k) -> c g k", g=PASSES)
         )
-        spread = keep.tile([P, PASSES, CHANNELS], BF16)
-        nc.vector.tensor_copy(
-            out=spread[:].rearrange("m g (k r) -> m g k r", r=2),
-            in_=ident[:].rearrange("m (k g) -> m g k", g=PASSES).unsqueeze(3).to_broadcast([P, PASSES, CHANNELS // 2, 2]),
-        )
-
         pixel = ident[:].rearrange("k (i j) -> k i j", j=COLS)
         three = keep.tile([P, OUT_ROWS, COLS + 2], BF16)
         nc.vector.memset(three[:, :, 0 : COLS + 2 : COLS + 1], 0.0)
@@ -92,148 +83,147 @@ def tile_qca_operator_deep_pa_kernel(tc, x_cat, w1_words, w1_scales, out):
         nc.vector.tensor_tensor(
             out=sides[:], in0=three[:, :, 0:COLS], in1=three[:, :, 2 : COLS + 2], op=ALU.add
         )
-        window = keep.tile([P, OUT_ROWS * COLS], BF16)
+        window = keep.tile([P, OUT_PIXELS], BF16)
         nc.vector.tensor_tensor(
             out=window[:].rearrange("k (i j) -> k i j", j=COLS), in0=sides[:], in1=two[:], op=ALU.add
         )
+        spread = keep.tile([P, PASSES, CHANNELS], BF16)
+        nc.vector.tensor_copy(
+            out=spread[:].rearrange("m g (k r) -> m g k r", r=2),
+            in_=ident[:].rearrange("m (k g) -> m g k", g=PASSES).unsqueeze(3).to_broadcast([P, PASSES, CHANNELS // 2, 2]),
+        )
 
-        x_turned = keep.tile([P, PIXEL_TILES, BLOCKS, P], BF16)
-        nbr = keep.tile([P, PIXEL_TILES, N_TILE], BF16)
-        xn_words = keep.tile([P, PIXEL_TILES, PASSES * N_TILE], U32, align_bytes=64)
-        xn_scales = keep.tile([P, PIXEL_TILES, PASSES * N_TILE], U8, align_bytes=64)
-        grouped_of = {}
+        x_turned_of, turned_of, summed_of, nbr_of, twice_of, grouped_of = {}, {}, {}, {}, {}, {}
+        words_of, scales_of = {}, {}
 
-        turned_of, summed_of = {}, {}
-
-        def turn(n, part, parts):
-            b, half = divmod(n, ROWS // TILE_ROWS)
-            top = TILE_ROWS * half
-            count = BLOCKS // parts
-            turned_of[n, part] = banks.tile([P, count, P], BF16, tag="bank", name="turned")
+        def turn(n):
+            b, top, rows = TILES[n]
+            count = rows // OUT_ROWS
+            turned_of[n] = banks.tile([P, count, P], BF16, tag="bank", name="turned")
             for i in range(count):
-                first = top + OUT_ROWS * (part * count + i)
+                start = top + OUT_ROWS * i
                 nc.tensor.transpose(
-                    turned_of[n, part][:, i, :],
-                    x_rows[:, b, first : first + BLOCK_ROWS, :].rearrange("c i j -> c (i j)"),
+                    turned_of[n][:, i, :],
+                    x_rows[:, b, start : start + BLOCK_ROWS, :].rearrange("c i j -> c (i j)"),
                     mixed[:],
                 )
 
-        def keep_turned(n, part, parts, copy):
-            count = BLOCKS // parts
+        def keep_turned(n, copy):
+            count = TILES[n][2] // OUT_ROWS
+            x_turned_of[n] = keep.tile([P, count, P], BF16, name="x_turned%d" % n)
             copy(
-                out=x_turned[:, n, part * count : (part + 1) * count, :]
-                .rearrange("k i c -> k (i c)")
-                .bitcast(F32),
-                in_=turned_of[n, part][:].rearrange("k i c -> k (i c)").bitcast(F32),
+                out=x_turned_of[n][:].rearrange("k i m -> k (i m)").bitcast(F32),
+                in_=turned_of[n][:].rearrange("k i m -> k (i m)").bitcast(F32),
             )
 
-        def sum_neighbours(n):
-            summed_of[n] = banks.tile([P, N_TILE], BF16, tag="bank", name="summed")
-            width = OUT_ROWS * COLS
-            for i in range(BLOCKS):
+        def sum_neighbours(n, times):
+            count = TILES[n][2] // OUT_ROWS
+            summed_of[n] = banks.tile([P, count * OUT_PIXELS * times], BF16, tag="bank", name="summed")
+            width = OUT_PIXELS * times
+            for i in range(count):
                 nc.tensor.matmul(
                     out=summed_of[n][:, width * i : width * (i + 1)],
-                    lhsT=x_turned[:, n, i, :],
-                    rhs=window[:],
+                    lhsT=x_turned_of[n][:, i, :],
+                    rhs=window[:] if times == 1 else window[:].unsqueeze(2).to_broadcast([P, OUT_PIXELS, times]),
                     start=True,
                     stop=True,
                 )
 
         def keep_summed(n, copy):
-            copy(out=nbr[:, n, :].bitcast(F32), in_=summed_of[n][:].bitcast(F32))
+            width = TILES[n][2] * COLS
+            nbr_of[n] = keep.tile([P, width], BF16, name="nbr%d" % n)
+            copy(out=nbr_of[n][:].bitcast(F32), in_=summed_of[n][:].bitcast(F32))
 
-        twice_of = {}
+        def spread_channels(n):
+            width = TILES[n][2] * COLS
+            for g in range(PASSES):
+                twice_of[n, g] = banks.tile([P, width, 2], BF16, tag="bank", name="twice")
+                for start in range(0, width, BANK // 2):
+                    pixels = slice(start, start + BANK // 2)
+                    nc.tensor.matmul(
+                        out=twice_of[n, g][:, pixels, :],
+                        lhsT=spread[:, g, :],
+                        rhs=nbr_of[n][:, pixels].unsqueeze(2).to_broadcast([P, BANK // 2, 2]),
+                        start=True,
+                        stop=True,
+                    )
 
-        def spread_channels(n, g):
-            twice_of[n, g] = banks.tile([P, N_TILE, 2], BF16, tag="bank", name="twice")
-            for h in range(2):
-                pixels = slice(h * N_TILE // 2, (h + 1) * N_TILE // 2)
-                nc.tensor.matmul(
-                    out=twice_of[n, g][:, pixels, :],
-                    lhsT=spread[:, g, :],
-                    rhs=nbr[:, n, pixels].unsqueeze(2).to_broadcast([P, N_TILE // 2, 2]),
-                    start=True,
-                    stop=True,
-                )
+        def grouped(n):
+            if n not in grouped_of:
+                width = TILES[n][2] * COLS
+                grouped_of[n] = keep.tile([P, PASSES, PACK * width], BF16, align_bytes=64, name="grouped%d" % n)
+            return grouped_of[n]
 
         def make_words(n, g, copy):
-            if g == 0:
-                grouped_of[n] = stage.tile([P, PASSES, PACK * N_TILE], BF16, align_bytes=64, name="grouped")
+            width = TILES[n][2] * COLS
             copy(
-                out=grouped_of[n][:, g, :].bitcast(F32).rearrange("p (w d) -> p w d", d=2),
-                in_=twice_of[n, g][:].bitcast(F32).to_broadcast([P, N_TILE, 2]),
+                out=grouped(n)[:, g, :].bitcast(F32).rearrange("p (w d) -> p w d", d=2),
+                in_=twice_of[n, g][:].rearrange("p w d -> p (w d)").bitcast(F32).unsqueeze(2).to_broadcast([P, width, 2]),
             )
 
-        def sum_neighbours_twice(n):
-            summed_of[n] = banks.tile([P, N_TILE, 2], BF16, tag="bank", name="summed")
-            width = OUT_ROWS * COLS
-            for i in range(BLOCKS):
-                nc.tensor.matmul(
-                    out=summed_of[n][:, width * i : width * (i + 1), :],
-                    lhsT=x_turned[:, n, i, :],
-                    rhs=window[:].unsqueeze(2).to_broadcast([P, width, 2]),
-                    start=True,
-                    stop=True,
-                )
-
         def move_words(n, copy):
-            grouped_of[n] = stage.tile([P, PASSES, PACK * N_TILE], BF16, align_bytes=64, name="grouped")
-            quads = stage.tile([P, PACK * N_TILE], BF16, name="quads")
+            width = TILES[n][2] * COLS
+            quads = keep.tile([P, PACK * width], BF16, name="quads%d" % n)
             copy(
                 out=quads[:].bitcast(F32).rearrange("m (w d) -> m w d", d=2),
-                in_=summed_of[n][:].bitcast(F32).to_broadcast([P, N_TILE, 2]),
+                in_=summed_of[n][:].bitcast(F32).unsqueeze(2).to_broadcast([P, width, 2]),
             )
             for g in range(PASSES):
                 for r in range(2):
-                    nc.sync.dma_start(out=grouped_of[n][r:P:2, g, :], in_=quads[g:P:2, :])
+                    nc.sync.dma_start(out=grouped(n)[r:P:2, g, :], in_=quads[g:P:2, :])
 
         def quantise(n):
+            width = TILES[n][2] * COLS
+            words_of[n] = keep.tile([P, PASSES * width], U32, align_bytes=64, name="xn_words%d" % n)
+            scales_of[n] = keep.tile([P, PASSES * width], U8, align_bytes=64, name="xn_scales%d" % n)
             nc.vector.quantize_mx(
-                out=xn_words[:, n, :].bitcast(FP8X4),
-                scales=xn_scales[:, n, :],
+                out=words_of[n][:].bitcast(FP8X4),
+                scales=scales_of[n][:],
                 in_=grouped_of[n][:].rearrange("p g c -> p (g c)"),
             )
 
-        def minus_one(exp_of_sums):
-            nc.gpsimd.tensor_scalar(
-                out=exp_of_sums, in0=exp_of_sums, scalar1=1.0, scalar2=-1.0, op0=ALU.mult, op1=ALU.add
-            )
+        def minus_one(exp_of_sums, on_scalar):
+            if on_scalar:
+                nc.scalar.activation(out=exp_of_sums, in_=exp_of_sums, func=ACT.Copy, bias=-1.0)
+            else:
+                nc.gpsimd.tensor_scalar(
+                    out=exp_of_sums, in0=exp_of_sums, scalar1=1.0, scalar2=-1.0, op0=ALU.mult, op1=ALU.add
+                )
 
-        def output_pair(n, pair, tile_by_tile):
-            while_quantising = pair == 0 and n in (1, 2)
-            b, half = divmod(n, ROWS // TILE_ROWS)
-            top = TILE_ROWS * half
-            exp_m1 = exps.tile([P, 2, N_TILE], F32)
+        def output_unit(n, part, on_scalar, final):
+            b, top, rows = TILES[n]
+            width = rows * COLS
+            side_by_side = BANK // width
+            exp_m1 = exps.tile([P, 2, BANK], F32)
             sums = []
             for t in range(2):
-                m = 2 * pair + t
-                acc = banks.tile([P, N_TILE], F32, tag="bank", name="acc")
-                for g in range(PASSES):
-                    nc.tensor.matmul_mx(
-                        out=acc[:],
-                        lhsT=w_words[:, g, 2 * P * m : 2 * P * (m + 1)].bitcast(FP4X4),
-                        lhsT_scale=w_scales[:, g, P * m : P * (m + 1)],
-                        rhs=xn_words[:, n, N_TILE * g : N_TILE * (g + 1)].bitcast(FP8X4),
-                        rhs_scale=xn_scales[:, n, N_TILE * g : N_TILE * (g + 1)],
-                        start=(g == 0),
-                        stop=(g == PASSES - 1),
-                    )
+                acc = banks.tile([P, BANK], F32, tag="bank", name="acc")
+                for s in range(side_by_side):
+                    m = side_by_side * (2 * part + t) + s
+                    step = BANK if width == BANK else 128
+                    for start in range(0, width, step):
+                        for g in range(PASSES):
+                            nc.tensor.matmul_mx(
+                                out=acc[:, width * s + start : width * s + start + step],
+                                lhsT=w_words[:, g, 2 * P * m : 2 * P * (m + 1)].bitcast(FP4X4),
+                                lhsT_scale=w_scales[:, g, P * m : P * (m + 1)],
+                                rhs=words_of[n][:, width * g + start : width * g + start + step].bitcast(FP8X4),
+                                rhs_scale=scales_of[n][:, width * g + start : width * g + start + step],
+                                start=(g == 0),
+                                stop=(g == PASSES - 1),
+                            )
                 nc.scalar.activation(out=exp_m1[:, t, :], in_=acc[:], func=ACT.Exp)
                 sums.append(acc)
-                if tile_by_tile:
-                    minus_one(exp_m1[:, t, :])
-            if while_quantising:
-                nc.scalar.activation(out=exp_m1[:], in_=exp_m1[:], func=ACT.Copy, bias=-1.0)
-            elif not tile_by_tile:
-                minus_one(exp_m1[:])
-            result = results.tile([P, 2, N_TILE], F32)
-            final_pair = (n, pair) == (PIXEL_TILES - 1, OUT_PAIRS - 1)
+                if final:
+                    minus_one(exp_m1[:, t, :], on_scalar)
+            if not final:
+                minus_one(exp_m1[:], on_scalar)
+            result = results.tile([P, 2, BANK], F32)
+            channels = 2 * side_by_side * P
             for t in range(2):
-                m = 2 * pair + t
-                pieces = 2 if final_pair and t == 1 else 1
-                rows = TILE_ROWS // pieces
+                pieces = 2 if final and t == 1 else 1
                 for piece in range(pieces):
-                    columns = slice(piece * rows * COLS, (piece + 1) * rows * COLS)
+                    columns = slice(piece * BANK // pieces, (piece + 1) * BANK // pieces)
                     nc.vector.scalar_tensor_tensor(
                         out=result[:, t, columns],
                         in0=sums[t][:, columns],
@@ -242,50 +232,62 @@ def tile_qca_operator_deep_pa_kernel(tc, x_cat, w1_words, w1_scales, out):
                         op0=ALU.max,
                         op1=ALU.min,
                     )
-                    if final_pair:
+                    if final:
+                        m = 2 * part + t
+                        piece_rows = rows // pieces
                         nc.sync.dma_start(
                             out=out[
-                                b, P * m : P * (m + 1), top + piece * rows : top + (piece + 1) * rows, :
+                                b, P * m : P * (m + 1), top + piece * piece_rows : top + (piece + 1) * piece_rows, :
                             ].rearrange("o i j -> o (i j)"),
                             in_=result[:, t, columns],
                         )
-            if not final_pair:
+            if not final:
                 nc.sync.dma_start(
-                    out=out[b, 2 * P * pair : 2 * P * (pair + 1), top : top + TILE_ROWS, :].rearrange(
-                        "(t o) i j -> o t (i j)", t=2
+                    out=out[b, channels * part : channels * (part + 1), top : top + rows, :].rearrange(
+                        "(q o) i j -> o q (i j)", o=P
                     ),
-                    in_=result[:],
+                    in_=result[:].rearrange("p t (s w) -> p (t s) w", w=width),
                 )
 
         scalar, vector = nc.scalar.copy, nc.vector.tensor_copy
-        turn(0, 0, 1)
-        turn(1, 0, 1)
-        turn(2, 0, 1)
-        keep_turned(0, 0, 1, scalar)
-        keep_turned(1, 0, 1, vector)
-        sum_neighbours(0)
-        turn(3, 0, 1)
-        keep_turned(2, 0, 1, scalar)
+        turn(0)
+        turn(1)
+        turn(2)
+        keep_turned(0, vector)
+        keep_turned(1, vector)
+        keep_turned(2, scalar)
+        sum_neighbours(0, 1)
+        sum_neighbours(1, 1)
+        turn(3)
         keep_summed(0, scalar)
-        sum_neighbours_twice(2)
-        spread_channels(0, 0)
-        spread_channels(0, 1)
-        keep_turned(3, 0, 1, vector)
-        move_words(2, vector)
-        make_words(0, 0, scalar)
-        sum_neighbours(1)
+        keep_turned(3, vector)
+        sum_neighbours(2, 1)
+        keep_summed(1, vector)
+        keep_summed(2, scalar)
+        spread_channels(0)
+        spread_channels(1)
+        spread_channels(2)
+        turn(4)
+        make_words(0, 0, vector)
         make_words(0, 1, vector)
         quantise(0)
-        sum_neighbours_twice(3)
-        keep_summed(1, scalar)
-        move_words(3, scalar)
-        spread_channels(1, 0)
-        spread_channels(1, 1)
-        make_words(1, 0, scalar)
-        make_words(1, 1, vector)
+        make_words(1, 1, scalar)
+        make_words(1, 0, vector)
         quantise(1)
-        for n in range(PIXEL_TILES):
-            for pair in range(OUT_PAIRS):
-                output_pair(n, pair, (n, pair) in ((0, 0), (PIXEL_TILES - 1, OUT_PAIRS - 1)))
-                if pair == 2 and n < AHEAD:
-                    quantise(n + AHEAD)
+        make_words(2, 0, scalar)
+        make_words(2, 1, scalar)
+        sum_neighbours(3, 2)
+        keep_turned(4, vector)
+        quantise(2)
+        move_words(3, vector)
+        units = [(n, part) for n in range(len(TILES)) for part in range(TILES[n][2] // 4)]
+        for i in range(UNITS):
+            n, part = units[i]
+            output_unit(n, part, i in (5, 10), i == UNITS - 1)
+            if i == 2:
+                sum_neighbours(4, 2)
+                move_words(4, scalar)
+            if i == 3:
+                quantise(3)
+            if i == 7:
+                quantise(4)

@@ -190,9 +190,8 @@ def tile_qca_operator_deep_pa_kernel(tc, x_cat, w1_words, w1_scales, out):
                     out=exp_of_sums, in0=exp_of_sums, scalar1=1.0, scalar2=-1.0, op0=ALU.mult, op1=ALU.add
                 )
 
-        def output_unit(n, part, on_scalar, final):
-            b, top, rows = TILES[n]
-            width = rows * COLS
+        def multiply(n, part, on_scalar, final):
+            width = TILES[n][2] * COLS
             side_by_side = BANK // width
             exp_m1 = exps.tile([P, 2, BANK], F32)
             sums = []
@@ -218,8 +217,13 @@ def tile_qca_operator_deep_pa_kernel(tc, x_cat, w1_words, w1_scales, out):
                     minus_one(exp_m1[:, t, :], on_scalar)
             if not final:
                 minus_one(exp_m1[:], on_scalar)
+            return sums, exp_m1
+
+        def finish(n, part, sums, exp_m1, final):
+            b, top, rows = TILES[n]
+            width = rows * COLS
             result = results.tile([P, 2, BANK], F32)
-            channels = 2 * side_by_side * P
+            channels = 2 * (BANK // width) * P
             for t in range(2):
                 pieces = 2 if final and t == 1 else 1
                 for piece in range(pieces):
@@ -254,39 +258,40 @@ def tile_qca_operator_deep_pa_kernel(tc, x_cat, w1_words, w1_scales, out):
         turn(1)
         turn(2)
         keep_turned(0, vector)
-        keep_turned(1, vector)
-        keep_turned(2, scalar)
+        keep_turned(1, scalar)
         sum_neighbours(0, 1)
         sum_neighbours(1, 1)
         turn(3)
-        keep_summed(0, scalar)
-        keep_turned(3, vector)
+        keep_turned(2, vector)
+        keep_summed(0, vector)
+        keep_summed(1, scalar)
         sum_neighbours(2, 1)
-        keep_summed(1, vector)
+        keep_turned(3, scalar)
         keep_summed(2, scalar)
         spread_channels(0)
-        spread_channels(1)
-        spread_channels(2)
-        turn(4)
-        make_words(0, 0, vector)
+        make_words(0, 0, scalar)
         make_words(0, 1, vector)
+        spread_channels(1)
         quantise(0)
-        make_words(1, 1, scalar)
-        make_words(1, 0, vector)
+        make_words(1, 0, scalar)
+        make_words(1, 1, vector)
+        turn(4)
         quantise(1)
+        keep_turned(4, scalar)
+        spread_channels(2)
         make_words(2, 0, scalar)
-        make_words(2, 1, scalar)
+        make_words(2, 1, vector)
         sum_neighbours(3, 2)
-        keep_turned(4, vector)
         quantise(2)
-        move_words(3, vector)
+        move_words(3, scalar)
+        sum_neighbours(4, 2)
+        move_words(4, vector)
         units = [(n, part) for n in range(len(TILES)) for part in range(TILES[n][2] // 4)]
         for i in range(UNITS):
             n, part = units[i]
-            output_unit(n, part, i in (5, 10), i == UNITS - 1)
-            if i == 2:
-                sum_neighbours(4, 2)
-                move_words(4, scalar)
+            final = i == UNITS - 1
+            sums, exp_m1 = multiply(n, part, i in (5, 9), final)
+            finish(n, part, sums, exp_m1, final)
             if i == 3:
                 quantise(3)
             if i == 7:

from contextlib import ExitStack

import concourse.mybir as mybir
from concourse.masks import make_identity

F32 = mybir.dt.float32
BF16 = mybir.dt.bfloat16
I32 = mybir.dt.int32
U8 = mybir.dt.uint8
U32 = mybir.dt.uint32
FP8X4 = mybir.dt.float8_e4m3fn_x4
FP4X4 = mybir.dt.float4_e2m1fn_x4
ALU = mybir.AluOpType
ACT = mybir.ActivationFunctionType

P = 128
PACK = 4
BATCH, CHANNELS, ROWS, COLS = 2, 128, 32, 32
PIXELS = BATCH * ROWS * COLS
HID = 1024
PASSES = 2
BLOCK_ROWS = P // COLS
OUT_ROWS = BLOCK_ROWS - 2
OUT_PIXELS = OUT_ROWS * COLS
BANK = 512
TILES = ((0, 0, 8), (0, 8, 8), (0, 16, 16), (1, 0, 16), (1, 16, 16))
UNITS = PIXELS * HID // (P * 2 * BANK)

FLOPS = 2 * PIXELS * PASSES * P * PACK * HID


def tile_qca_operator_deep_pa_kernel(tc, x_cat, w1_words, w1_scales, out):
    nc = tc.nc
    with ExitStack() as ctx:
        ctx.enter_context(tc.manual_schedule())
        keep = ctx.enter_context(tc.tile_pool(name="keep", bufs=1))
        exps = ctx.enter_context(tc.tile_pool(name="exps", bufs=6))
        results = ctx.enter_context(tc.tile_pool(name="results", bufs=8))
        banks = ctx.enter_context(tc.psum_pool(name="banks", bufs=8))

        ident = keep.tile([P, P], BF16)
        make_identity(nc, ident[:])
        zeros = keep.tile([P, P], BF16)
        nc.vector.memset(zeros[:], 0.0)
        x_rows = keep.tile([P, BATCH, ROWS + 2, COLS], BF16)
        nc.vector.memset(x_rows[:, :, 0 : ROWS + 2 : ROWS + 1, :], 0.0)
        first = 17
        nc.sync.dma_start(out=x_rows[:, 0, 1 : first + 1, :], in_=x_cat[0, :, 0:first, :])
        nc.sync.dma_start(out=x_rows[:, 0, first + 1 : ROWS + 1, :], in_=x_cat[0, :, first:ROWS, :])
        nc.sync.dma_start(out=x_rows[:, 1, 1 : ROWS + 1, :], in_=x_cat[1])

        w_words = keep.tile([P, PASSES, 2 * HID], U8, align_bytes=64)
        for g in range(PASSES):
            nc.sync.dma_start(out=w_words[:, g, :].bitcast(I32), in_=w1_words[g].bitcast(I32))

        w_scales = keep.tile([P, PASSES, HID], U8, align_bytes=64)
        nc.gpsimd.memset(w_scales[:].bitcast(I32), 0)
        for quadrant in range(4):
            nc.sync.dma_start(
                out=w_scales[32 * quadrant : 32 * quadrant + 4, :, :].bitcast(I32),
                in_=w1_scales[:, 4 * quadrant : 4 * quadrant + 4, :].bitcast(I32).rearrange("g r n -> r g n"),
            )

        warm = keep.tile([P, 1], F32)
        nc.vector.memset(warm[:], 0.0)
        nc.scalar.activation(out=warm[:], in_=warm[:], func=ACT.Exp)

        idle = banks.tile([P, BANK], F32, tag="bank", name="idle")
        for w in range(3):
            nc.tensor.matmul(out=idle[:], lhsT=zeros[:], rhs=zeros[:, 0:1].to_broadcast([P, BANK]), start=True, stop=True)

        mixed = keep.tile([P, P], BF16)
        nc.vector.tensor_copy(
            out=mixed[:].rearrange("c (k g) -> c g k", g=PASSES), in_=ident[:].rearrange("c (g k) -> c g k", g=PASSES)
        )
        pixel = ident[:].rearrange("k (i j) -> k i j", j=COLS)
        three = keep.tile([P, OUT_ROWS, COLS + 2], BF16)
        nc.vector.memset(three[:, :, 0 : COLS + 2 : COLS + 1], 0.0)
        two = keep.tile([P, OUT_ROWS, COLS], BF16)
        nc.vector.tensor_tensor(out=two[:], in0=pixel[:, 0:2, :], in1=pixel[:, 2:4, :], op=ALU.add)
        nc.vector.tensor_tensor(out=three[:, :, 1 : COLS + 1], in0=two[:], in1=pixel[:, 1:3, :], op=ALU.add)
        sides = keep.tile([P, OUT_ROWS, COLS], BF16)
        nc.vector.tensor_tensor(
            out=sides[:], in0=three[:, :, 0:COLS], in1=three[:, :, 2 : COLS + 2], op=ALU.add
        )
        window = keep.tile([P, OUT_PIXELS], BF16)
        nc.vector.tensor_tensor(
            out=window[:].rearrange("k (i j) -> k i j", j=COLS), in0=sides[:], in1=two[:], op=ALU.add
        )
        spread = keep.tile([P, PASSES, CHANNELS], BF16)
        nc.vector.tensor_copy(
            out=spread[:].rearrange("m g (k r) -> m g k r", r=2),
            in_=ident[:].rearrange("m (k g) -> m g k", g=PASSES).unsqueeze(3).to_broadcast([P, PASSES, CHANNELS // 2, 2]),
        )

        x_turned_of, turned_of, summed_of, nbr_of, twice_of, grouped_of = {}, {}, {}, {}, {}, {}
        words_of, scales_of = {}, {}

        def turn(n):
            b, top, rows = TILES[n]
            count = rows // OUT_ROWS
            turned_of[n] = banks.tile([P, count, P], BF16, tag="bank", name="turned")
            for i in range(count):
                start = top + OUT_ROWS * i
                nc.tensor.transpose(
                    turned_of[n][:, i, :],
                    x_rows[:, b, start : start + BLOCK_ROWS, :].rearrange("c i j -> c (i j)"),
                    mixed[:],
                )

        def keep_turned(n, copy):
            count = TILES[n][2] // OUT_ROWS
            x_turned_of[n] = keep.tile([P, count, P], BF16, name="x_turned%d" % n)
            copy(
                out=x_turned_of[n][:].rearrange("k i m -> k (i m)").bitcast(F32),
                in_=turned_of[n][:].rearrange("k i m -> k (i m)").bitcast(F32),
            )

        def sum_neighbours(n, times):
            count = TILES[n][2] // OUT_ROWS
            summed_of[n] = banks.tile([P, count * OUT_PIXELS * times], BF16, tag="bank", name="summed")
            width = OUT_PIXELS * times
            for i in range(count):
                nc.tensor.matmul(
                    out=summed_of[n][:, width * i : width * (i + 1)],
                    lhsT=x_turned_of[n][:, i, :],
                    rhs=window[:] if times == 1 else window[:].unsqueeze(2).to_broadcast([P, OUT_PIXELS, times]),
                    start=True,
                    stop=True,
                )

        def keep_summed(n, copy):
            width = TILES[n][2] * COLS
            nbr_of[n] = keep.tile([P, width], BF16, name="nbr%d" % n)
            copy(out=nbr_of[n][:].bitcast(F32), in_=summed_of[n][:].bitcast(F32))

        def spread_channels(n):
            width = TILES[n][2] * COLS
            for g in range(PASSES):
                twice_of[n, g] = banks.tile([P, width, 2], BF16, tag="bank", name="twice")
                for start in range(0, width, BANK // 2):
                    pixels = slice(start, start + BANK // 2)
                    nc.tensor.matmul(
                        out=twice_of[n, g][:, pixels, :],
                        lhsT=spread[:, g, :],
                        rhs=nbr_of[n][:, pixels].unsqueeze(2).to_broadcast([P, BANK // 2, 2]),
                        start=True,
                        stop=True,
                    )

        def grouped(n):
            if n not in grouped_of:
                width = TILES[n][2] * COLS
                grouped_of[n] = keep.tile([P, PASSES, PACK * width], BF16, align_bytes=64, name="grouped%d" % n)
            return grouped_of[n]

        def make_words(n, g, copy):
            width = TILES[n][2] * COLS
            copy(
                out=grouped(n)[:, g, :].bitcast(F32).rearrange("p (w d) -> p w d", d=2),
                in_=twice_of[n, g][:].rearrange("p w d -> p (w d)").bitcast(F32).unsqueeze(2).to_broadcast([P, width, 2]),
            )

        def move_words(n, copy):
            width = TILES[n][2] * COLS
            quads = keep.tile([P, PACK * width], BF16, name="quads%d" % n)
            copy(
                out=quads[:].bitcast(F32).rearrange("m (w d) -> m w d", d=2),
                in_=summed_of[n][:].bitcast(F32).unsqueeze(2).to_broadcast([P, width, 2]),
            )
            for g in range(PASSES):
                for r in range(2):
                    nc.sync.dma_start(out=grouped(n)[r:P:2, g, :], in_=quads[g:P:2, :])

        def quantise(n):
            width = TILES[n][2] * COLS
            words_of[n] = keep.tile([P, PASSES * width], U32, align_bytes=64, name="xn_words%d" % n)
            scales_of[n] = keep.tile([P, PASSES * width], U8, align_bytes=64, name="xn_scales%d" % n)
            nc.vector.quantize_mx(
                out=words_of[n][:].bitcast(FP8X4),
                scales=scales_of[n][:],
                in_=grouped_of[n][:].rearrange("p g c -> p (g c)"),
            )

        def minus_one(exp_of_sums, on_scalar):
            if on_scalar:
                nc.scalar.activation(out=exp_of_sums, in_=exp_of_sums, func=ACT.Copy, bias=-1.0)
            else:
                nc.gpsimd.tensor_scalar(
                    out=exp_of_sums, in0=exp_of_sums, scalar1=1.0, scalar2=-1.0, op0=ALU.mult, op1=ALU.add
                )

        def multiply(n, part, on_scalar, final):
            width = TILES[n][2] * COLS
            side_by_side = BANK // width
            exp_m1 = exps.tile([P, 2, BANK], F32)
            sums = []
            for t in range(2):
                acc = banks.tile([P, BANK], F32, tag="bank", name="acc")
                for s in range(side_by_side):
                    m = side_by_side * (2 * part + t) + s
                    step = BANK if width == BANK else 128
                    for start in range(0, width, step):
                        for g in range(PASSES):
                            nc.tensor.matmul_mx(
                                out=acc[:, width * s + start : width * s + start + step],
                                lhsT=w_words[:, g, 2 * P * m : 2 * P * (m + 1)].bitcast(FP4X4),
                                lhsT_scale=w_scales[:, g, P * m : P * (m + 1)],
                                rhs=words_of[n][:, width * g + start : width * g + start + step].bitcast(FP8X4),
                                rhs_scale=scales_of[n][:, width * g + start : width * g + start + step],
                                start=(g == 0),
                                stop=(g == PASSES - 1),
                            )
                nc.scalar.activation(out=exp_m1[:, t, :], in_=acc[:], func=ACT.Exp)
                sums.append(acc)
                if final:
                    minus_one(exp_m1[:, t, :], on_scalar)
            if not final:
                minus_one(exp_m1[:], on_scalar)
            return sums, exp_m1

        def finish(n, part, sums, exp_m1, final):
            b, top, rows = TILES[n]
            width = rows * COLS
            result = results.tile([P, 2, BANK], F32)
            channels = 2 * (BANK // width) * P
            for t in range(2):
                pieces = 2 if final and t == 1 else 1
                for piece in range(pieces):
                    columns = slice(piece * BANK // pieces, (piece + 1) * BANK // pieces)
                    nc.vector.scalar_tensor_tensor(
                        out=result[:, t, columns],
                        in0=sums[t][:, columns],
                        scalar=0.0,
                        in1=exp_m1[:, t, columns],
                        op0=ALU.max,
                        op1=ALU.min,
                    )
                    if final:
                        m = 2 * part + t
                        piece_rows = rows // pieces
                        nc.sync.dma_start(
                            out=out[
                                b, P * m : P * (m + 1), top + piece * piece_rows : top + (piece + 1) * piece_rows, :
                            ].rearrange("o i j -> o (i j)"),
                            in_=result[:, t, columns],
                        )
            if not final:
                nc.sync.dma_start(
                    out=out[b, channels * part : channels * (part + 1), top : top + rows, :].rearrange(
                        "(q o) i j -> o q (i j)", o=P
                    ),
                    in_=result[:].rearrange("p t (s w) -> p (t s) w", w=width),
                )

        scalar, vector = nc.scalar.copy, nc.vector.tensor_copy
        turn(0)
        turn(1)
        turn(2)
        keep_turned(0, vector)
        keep_turned(1, scalar)
        sum_neighbours(0, 1)
        sum_neighbours(1, 1)
        turn(3)
        keep_turned(2, vector)
        keep_summed(0, vector)
        keep_summed(1, scalar)
        sum_neighbours(2, 1)
        keep_turned(3, scalar)
        keep_summed(2, scalar)
        spread_channels(0)
        make_words(0, 0, scalar)
        make_words(0, 1, vector)
        spread_channels(1)
        quantise(0)
        make_words(1, 0, scalar)
        make_words(1, 1, vector)
        turn(4)
        quantise(1)
        keep_turned(4, scalar)
        spread_channels(2)
        make_words(2, 0, scalar)
        make_words(2, 1, vector)
        sum_neighbours(3, 2)
        quantise(2)
        move_words(3, scalar)
        sum_neighbours(4, 2)
        move_words(4, vector)
        units = [(n, part) for n in range(len(TILES)) for part in range(TILES[n][2] // 4)]
        for i in range(UNITS):
            n, part = units[i]
            final = i == UNITS - 1
            sums, exp_m1 = multiply(n, part, i in (5, 9), final)
            finish(n, part, sums, exp_m1, final)
            if i == 3:
                quantise(3)
            if i == 7:
                quantise(4)
